import numpy as np
import ml_dtypes


def mxq(x, axis, fmt="e4m3"):
    dtype, down = {"e4m3": (ml_dtypes.float8_e4m3fn, 7), "e5m2": (ml_dtypes.float8_e5m2, 14)}[fmt]
    v = np.moveaxis(np.asarray(x, np.float32).astype(ml_dtypes.bfloat16).astype(np.float64), axis, -1)
    blocks = v.reshape(v.shape[:-1] + (-1, 32))
    amax = np.abs(blocks).max(-1, keepdims=True)
    byte = np.maximum(np.where(amax > 0, np.frexp(amax)[1] - 1 + 127, 0) - down, 1)
    scale = np.exp2(byte - 127.0)
    codes = (blocks / scale).astype(np.float32).astype(dtype).astype(np.float64)
    return np.moveaxis((codes * scale).reshape(v.shape), -1, axis)


WIDE = False


def mx_kscale(k):
    if not WIDE:
        return np.ones(k)
    levels = np.array([10, -10, 5, -5, 0])
    if k % 512:
        return np.exp2(np.random.permutation(np.resize(levels, k // 32))).repeat(32)
    a = np.empty((k // 512, 16))
    for p in range(k // 512):
        a[p, :8] = np.random.permutation(np.resize(levels, 8))
        for g in range(8):
            far = levels[np.abs(levels - a[p, g]) >= 10]
            a[p, g + 8] = far[np.random.randint(len(far))]
    return np.exp2(a.ravel()).repeat(32)


BF16 = ml_dtypes.bfloat16


def bf(x):
    return np.asarray(x, np.float32).astype(BF16)


def f64(x):
    return np.asarray(x).astype(np.float64)


B, N, T, D, DO, H, E = 128, 2, 32, 1024, 128, 8, 128
S = N * T


def sigmoid(v):
    return 1.0 / (1.0 + np.exp(-v))


def setup_inputs():
    r = np.random.standard_normal
    s = mx_kscale(D)
    return {
        "x": bf(r((B, S, D)) * s),
        "edge_features": bf(r((B, E))),
        "Wv": bf(r((D, DO)) / np.sqrt(D) / s[:, None]),
        "bv": bf(r(DO) * 0.3),
        "Wgate": bf(r((E, DO)) / np.sqrt(E)),
        "bgate": bf(r(DO) * 0.3),
        "Wscale": bf(r((E, DO)) * 0.7 / np.sqrt(E)),
        "bscale": bf(r(DO) * 0.3),
        "Wshift": bf(r((E, DO)) * 0.7 / np.sqrt(E)),
        "bshift": bf(r(DO) * 0.3),
    }


def reference(x, edge_features, Wv, bv, Wgate, bgate, Wscale, bscale, Wshift, bshift):
    e = f64(edge_features)
    v = (mxq(f64(x).reshape(B * S, D), 1, "e4m3") @ mxq(f64(Wv), 0, "e4m3")).reshape(B, S, DO) + f64(bv)
    gate = sigmoid(e @ f64(Wgate) + f64(bgate))
    scale = np.tanh(e @ f64(Wscale) + f64(bscale))
    shift = e @ f64(Wshift) + f64(bshift)
    return (v * (1.0 + scale[:, None, :]) + shift[:, None, :]) * gate[:, None, :]

@@ -1,0 +1,210 @@
+from contextlib import ExitStack
+
+import concourse.mybir as mybir
+from concourse.masks import make_identity
+
+F32 = mybir.dt.float32
+BF16 = mybir.dt.bfloat16
+U32 = mybir.dt.uint32
+U8 = mybir.dt.uint8
+FP8X4 = mybir.dt.float8_e4m3fn_x4
+ACT = mybir.ActivationFunctionType
+ALU = mybir.AluOpType
+
+P = 128
+ROWS = 64
+D = 1024
+DO = 128
+E = 128
+
+PACK = 4
+PASSES = D // (P * PACK)
+PAIRS = 2
+WORD_BLOCKS = PASSES * PAIRS
+
+LOAD_ROWS = 4
+LOADS = ROWS // LOAD_ROWS
+BANK_ROWS = 4
+BANKS = ROWS // BANK_ROWS
+UNIT_ROWS = 2
+UNITS = ROWS // UNIT_ROWS
+UNITS_PER_LOAD = LOAD_ROWS // UNIT_ROWS
+UNITS_PER_BANK = BANK_ROWS // UNIT_ROWS
+XT_BANKS = 6
+ACC_BANKS = 2
+LEAD = XT_BANKS // UNIT_ROWS
+
+FLOPS = 2 * P * ROWS * D * DO + 3 * 2 * P * E * DO
+
+
+def tile_graphditunit_pa_t_kernel(
+    tc, x, edge_features, Wv, bv, Wgate, bgate, Wscale, bscale, Wshift, bshift, out
+):
+    nc = tc.nc
+    with ExitStack() as ctx:
+        ctx.enter_context(tc.manual_schedule())
+        consts = ctx.enter_context(tc.tile_pool(name="consts", bufs=1))
+        x_pool = ctx.enter_context(tc.tile_pool(name="x_pool", bufs=LOADS))
+        rows_pool = ctx.enter_context(tc.tile_pool(name="rows_pool", bufs=BANKS))
+        unit_pool = ctx.enter_context(tc.tile_pool(name="unit_pool", bufs=LEAD + 2))
+        xt_pool = ctx.enter_context(tc.psum_pool(name="xt_pool", bufs=XT_BANKS))
+        acc_pool = ctx.enter_context(tc.psum_pool(name="acc_pool", bufs=ACC_BANKS))
+
+        ident_f32 = consts.tile([P, P], F32)
+        make_identity(nc, ident_f32[:])
+        ident_bf16 = consts.tile([P, P], BF16)
+        ones = consts.tile([P, P], BF16)
+        mod_w = consts.tile([P, 4, DO], BF16)
+        mod_b = consts.tile([P, 4, DO], BF16)
+        nc.vector.memset(mod_b[:], 0.0)
+        nc.vector.memset(mod_w[:, 3, :], 0.0)
+        nc.vector.memset(ones[:], 1.0)
+        nc.vector.tensor_copy(out=ident_bf16[:], in_=ident_f32[:])
+        table_warmer = consts.tile([P, 1], F32)
+        nc.scalar.activation(out=table_warmer[:], in_=ident_f32[:, 0:1], func=ACT.Sigmoid)
+
+        x_tiles = []
+
+        def load_x(c):
+            first = c * LOAD_ROWS
+            x_sb = x_pool.tile([P, LOAD_ROWS, D], BF16)
+            nc.sync.dma_start(out=x_sb[:], in_=x[:, first : first + LOAD_ROWS, :])
+            x_tiles.append(x_sb)
+
+        e_sb = consts.tile([P, E], BF16)
+        nc.sync.dma_start(out=e_sb[:], in_=edge_features[:, :])
+        load_x(0)
+        w_raw = consts.tile([P, PASSES, PACK, DO], BF16)
+        nc.sync.dma_start(
+            out=w_raw[:].rearrange("q g t d -> q g (t d)"),
+            in_=Wv.rearrange("(g q t) d -> q g (t d)", g=PASSES, t=PACK),
+        )
+        load_x(1)
+        nc.sync.dma_start(out=mod_w[:, 0, :], in_=Wgate[:, :])
+        nc.sync.dma_start(out=mod_w[:, 1, :], in_=Wscale[:, :])
+        nc.sync.dma_start(out=mod_w[:, 2, :], in_=Wshift[:, :])
+        for c in range(2, LOADS):
+            load_x(c)
+        for j, bias in enumerate((bgate, bscale, bshift, bv)):
+            nc.gpsimd.dma_start(out=mod_b[0:1, j, :], in_=bias.unsqueeze(0))
+
+        eT_ps = acc_pool.tile([P, P], BF16, tag="acc")
+        nc.tensor.transpose(eT_ps[:], e_sb[:], ident_bf16[:])
+        eT = consts.tile([P, P], BF16)
+        nc.vector.tensor_copy(out=eT[:], in_=eT_ps[:])
+
+        w_grouped = consts.tile([P, PASSES, DO, PACK], BF16, align_bytes=64)
+        w_codes = consts.tile([P, PASSES, DO], U32, align_bytes=64)
+        w_scales = consts.tile([P, PASSES, DO], U8, align_bytes=64)
+        nc.vector.tensor_copy(out=w_grouped[:], in_=w_raw[:].rearrange("q g t d -> q g d t"))
+        nc.vector.quantize_mx(
+            out=w_codes[:].rearrange("q g d -> q (g d)").bitcast(FP8X4),
+            scales=w_scales[:].rearrange("q g d -> q (g d)"),
+            in_=w_grouped[:].rearrange("q g d t -> q (g d t)"),
+        )
+
+        grouped_tiles = {}
+        quantised = {}
+
+        def transpose_unit(u):
+            x_words = x_tiles[u // UNITS_PER_LOAD][:].bitcast(F32)
+            grouped = unit_pool.tile([P, UNIT_ROWS, PASSES, P, PACK], BF16, align_bytes=64)
+            grouped_words = grouped[:].bitcast(F32)
+            for r in range(UNIT_ROWS):
+                row = (u % UNITS_PER_LOAD) * UNIT_ROWS + r
+                xt = xt_pool.tile([P, WORD_BLOCKS, P], F32)
+                for j in range(WORD_BLOCKS):
+                    g, h = divmod(j, PAIRS)
+                    first = g * PAIRS * P + h
+                    nc.tensor.transpose(
+                        xt[:, j, :],
+                        x_words[:, row, first : (g + 1) * PAIRS * P : PAIRS],
+                        ident_f32[:],
+                    )
+                nc.scalar.copy(
+                    out=grouped_words[:, r],
+                    in_=xt[:].rearrange("q (g h) b -> q g b h", g=PASSES),
+                )
+            grouped_tiles[u] = grouped
+
+        def quantise_unit(u):
+            codes = unit_pool.tile([P, UNIT_ROWS, PASSES, P], U32, align_bytes=64)
+            scales = unit_pool.tile([P, UNIT_ROWS, PASSES, P], U8, align_bytes=64)
+            nc.vector.quantize_mx(
+                out=codes[:].rearrange("q r g b -> q (r g b)").bitcast(FP8X4),
+                scales=scales[:].rearrange("q r g b -> q (r g b)"),
+                in_=grouped_tiles[u][:].rearrange("q r g b t -> q (r g b t)"),
+            )
+            quantised[u] = (codes, scales)
+
+        def multiply_unit(u, acc):
+            codes, scales = quantised[u]
+            for r in range(UNIT_ROWS):
+                bank_row = (u % UNITS_PER_BANK) * UNIT_ROWS + r
+                for g in range(PASSES):
+                    nc.tensor.matmul_mx(
+                        out=acc[:, bank_row, :],
+                        lhsT=codes[:, r, g, :].bitcast(FP8X4),
+                        lhsT_scale=scales[:, r, g, :],
+                        rhs=w_codes[:, g, :].bitcast(FP8X4),
+                        rhs_scale=w_scales[:, g, :],
+                        start=(g == 0),
+                        stop=(g == PASSES - 1),
+                    )
+
+        for u in range(LEAD):
+            transpose_unit(u)
+            quantise_unit(u)
+
+        mod_ps = acc_pool.tile([P, 4, DO], F32, tag="acc")
+        mod_flat = mod_ps[:].rearrange("b j d -> b (j d)")
+        nc.tensor.matmul(
+            mod_flat, lhsT=eT[:], rhs=mod_w[:].rearrange("k j d -> k (j d)"), start=True, stop=False
+        )
+        nc.tensor.matmul(
+            mod_flat, lhsT=ones[:], rhs=mod_b[:].rearrange("k j d -> k (j d)"), start=False, stop=True
+        )
+        gate = consts.tile([P, DO], F32)
+        scale = consts.tile([P, DO], F32)
+        nc.scalar.activation(out=gate[:], in_=mod_ps[:, 0, :], func=ACT.Sigmoid)
+        nc.scalar.activation(out=scale[:], in_=mod_ps[:, 1, :], func=ACT.Tanh)
+        factor = consts.tile([P, DO], F32)
+        shift_gate = consts.tile([P, DO], F32)
+        offset = consts.tile([P, DO], F32)
+        nc.vector.scalar_tensor_tensor(
+            out=factor[:], in0=scale[:], scalar=1.0, in1=gate[:], op0=ALU.add, op1=ALU.mult
+        )
+        nc.vector.tensor_tensor(out=shift_gate[:], in0=mod_ps[:, 2, :], in1=gate[:], op=ALU.mult)
+        nc.vector.tensor_tensor(out=offset[:], in0=mod_ps[:, 3, :], in1=factor[:], op=ALU.mult)
+        nc.vector.tensor_tensor(out=offset[:], in0=offset[:], in1=shift_gate[:], op=ALU.add)
+        factor_rows = factor[:].unsqueeze(1).to_broadcast([P, BANK_ROWS, DO])
+        offset_rows = offset[:].unsqueeze(1).to_broadcast([P, BANK_ROWS, DO])
+
+        rows_tiles = {}
+
+        def scale_bank(k, acc):
+            rows = rows_pool.tile([P, BANK_ROWS, DO], F32)
+            nc.vector.tensor_tensor(out=rows[:], in0=acc[:], in1=factor_rows, op=ALU.mult)
+            rows_tiles[k] = rows
+
+        def shift_and_store_bank(k):
+            rows = rows_tiles[k]
+            nc.vector.tensor_tensor(out=rows[:], in0=rows[:], in1=offset_rows, op=ALU.add)
+            nc.sync.dma_start(out=out[:, k * BANK_ROWS : (k + 1) * BANK_ROWS, :], in_=rows[:])
+
+        acc = None
+        for u in range(UNITS):
+            ahead = u + LEAD
+            k, part = divmod(u, UNITS_PER_BANK)
+            if ahead < UNITS:
+                transpose_unit(ahead)
+            if part == 0:
+                acc = acc_pool.tile([P, BANK_ROWS, DO], F32, tag="acc")
+            multiply_unit(u, acc)
+            if part == UNITS_PER_BANK - 1:
+                if k > 0:
+                    shift_and_store_bank(k - 1)
+                scale_bank(k, acc)
+            if ahead < UNITS:
+                quantise_unit(ahead)
+        shift_and_store_bank(BANKS - 1)

@@ -201,10 +201,11 @@ def tile_graphditunit_pa_t_kernel(
             if part == 0:
                 acc = acc_pool.tile([P, BANK_ROWS, DO], F32, tag="acc")
             multiply_unit(u, acc)
+            if part == 0 and 0 < k < BANKS - 1:
+                shift_and_store_bank(k - 1)
             if part == UNITS_PER_BANK - 1:
-                if k > 0:
-                    shift_and_store_bank(k - 1)
                 scale_bank(k, acc)
             if ahead < UNITS:
                 quantise_unit(ahead)
+        shift_and_store_bank(BANKS - 2)
         shift_and_store_bank(BANKS - 1)

@@ -23,12 +23,13 @@ PAIRS = 2
 WORD_BLOCKS = PASSES * PAIRS
 
 LOAD_ROWS = 4
-LOADS = ROWS // LOAD_ROWS
+SMALL_ROWS = 2
+SMALL_LOADS = 4
+LARGE_LOADS = (ROWS - SMALL_LOADS * SMALL_ROWS) // LOAD_ROWS
 BANK_ROWS = 4
 BANKS = ROWS // BANK_ROWS
 UNIT_ROWS = 2
 UNITS = ROWS // UNIT_ROWS
-UNITS_PER_LOAD = LOAD_ROWS // UNIT_ROWS
 UNITS_PER_BANK = BANK_ROWS // UNIT_ROWS
 XT_BANKS = 6
 ACC_BANKS = 2
@@ -44,7 +45,7 @@ def tile_graphditunit_pa_t_kernel(
     with ExitStack() as ctx:
         ctx.enter_context(tc.manual_schedule())
         consts = ctx.enter_context(tc.tile_pool(name="consts", bufs=1))
-        x_pool = ctx.enter_context(tc.tile_pool(name="x_pool", bufs=LOADS))
+        x_pool = ctx.enter_context(tc.tile_pool(name="x_pool", bufs=1))
         rows_pool = ctx.enter_context(tc.tile_pool(name="rows_pool", bufs=BANKS))
         unit_pool = ctx.enter_context(tc.tile_pool(name="unit_pool", bufs=LEAD + 2))
         xt_pool = ctx.enter_context(tc.psum_pool(name="xt_pool", bufs=XT_BANKS))
@@ -63,56 +64,48 @@ def tile_graphditunit_pa_t_kernel(
         table_warmer = consts.tile([P, 1], F32)
         nc.scalar.activation(out=table_warmer[:], in_=ident_f32[:, 0:1], func=ACT.Sigmoid)
 
-        x_tiles = []
+        x_rows = {}
 
-        def load_x(c):
-            first = c * LOAD_ROWS
-            x_sb = x_pool.tile([P, LOAD_ROWS, D], BF16)
-            nc.sync.dma_start(out=x_sb[:], in_=x[:, first : first + LOAD_ROWS, :])
-            x_tiles.append(x_sb)
+        def load_x(first, rows):
+            x_sb = x_pool.tile([P, rows, D], BF16, tag="x%d" % rows, bufs=SMALL_LOADS if rows == SMALL_ROWS else LARGE_LOADS)
+            nc.sync.dma_start(out=x_sb[:], in_=x[:, first : first + rows, :])
+            for r in range(rows):
+                x_rows[first + r] = (x_sb, r)
 
-        e_sb = consts.tile([P, E], BF16)
-        nc.sync.dma_start(out=e_sb[:], in_=edge_features[:, :])
-        load_x(0)
+        load_x(0, SMALL_ROWS)
+        load_x(SMALL_ROWS, SMALL_ROWS)
         w_raw = consts.tile([P, PASSES, PACK, DO], BF16)
         nc.sync.dma_start(
             out=w_raw[:].rearrange("q g t d -> q g (t d)"),
             in_=Wv.rearrange("(g q t) d -> q g (t d)", g=PASSES, t=PACK),
         )
-        load_x(1)
+        load_x(2 * SMALL_ROWS, SMALL_ROWS)
+        load_x(3 * SMALL_ROWS, SMALL_ROWS)
+        e_sb = consts.tile([P, E], BF16)
+        nc.sync.dma_start(out=e_sb[:], in_=edge_features[:, :])
         nc.sync.dma_start(out=mod_w[:, 0, :], in_=Wgate[:, :])
         nc.sync.dma_start(out=mod_w[:, 1, :], in_=Wscale[:, :])
         nc.sync.dma_start(out=mod_w[:, 2, :], in_=Wshift[:, :])
-        for c in range(2, LOADS):
-            load_x(c)
+        for first in range(SMALL_LOADS * SMALL_ROWS, ROWS, LOAD_ROWS):
+            load_x(first, LOAD_ROWS)
         for j, bias in enumerate((bgate, bscale, bshift, bv)):
             nc.gpsimd.dma_start(out=mod_b[0:1, j, :], in_=bias.unsqueeze(0))
-
-        eT_ps = acc_pool.tile([P, P], BF16, tag="acc")
-        nc.tensor.transpose(eT_ps[:], e_sb[:], ident_bf16[:])
-        eT = consts.tile([P, P], BF16)
-        nc.vector.tensor_copy(out=eT[:], in_=eT_ps[:])
 
         w_grouped = consts.tile([P, PASSES, DO, PACK], BF16, align_bytes=64)
         w_codes = consts.tile([P, PASSES, DO], U32, align_bytes=64)
         w_scales = consts.tile([P, PASSES, DO], U8, align_bytes=64)
         nc.vector.tensor_copy(out=w_grouped[:], in_=w_raw[:].rearrange("q g t d -> q g d t"))
-        nc.vector.quantize_mx(
-            out=w_codes[:].rearrange("q g d -> q (g d)").bitcast(FP8X4),
-            scales=w_scales[:].rearrange("q g d -> q (g d)"),
-            in_=w_grouped[:].rearrange("q g d t -> q (g d t)"),
-        )
 
         grouped_tiles = {}
         quantised = {}
 
         def transpose_unit(u):
-            x_words = x_tiles[u // UNITS_PER_LOAD][:].bitcast(F32)
             grouped = unit_pool.tile([P, UNIT_ROWS, PASSES, P, PACK], BF16, align_bytes=64)
             grouped_words = grouped[:].bitcast(F32)
             for r in range(UNIT_ROWS):
-                row = (u % UNITS_PER_LOAD) * UNIT_ROWS + r
-                xt = xt_pool.tile([P, WORD_BLOCKS, P], F32)
+                x_sb, row = x_rows[u * UNIT_ROWS + r]
+                x_words = x_sb[:].bitcast(F32)
+                xt = xt_pool.tile([P, WORD_BLOCKS, P], F32, tag="xt")
                 for j in range(WORD_BLOCKS):
                     g, h = divmod(j, PAIRS)
                     first = g * PAIRS * P + h
@@ -155,30 +148,45 @@ def tile_graphditunit_pa_t_kernel(
         for u in range(LEAD):
             transpose_unit(u)
             quantise_unit(u)
+            if u == 0:
+                nc.vector.quantize_mx(
+                    out=w_codes[:].rearrange("q g d -> q (g d)").bitcast(FP8X4),
+                    scales=w_scales[:].rearrange("q g d -> q (g d)"),
+                    in_=w_grouped[:].rearrange("q g d t -> q (g d t)"),
+                )
 
-        mod_ps = acc_pool.tile([P, 4, DO], F32, tag="acc")
-        mod_flat = mod_ps[:].rearrange("b j d -> b (j d)")
-        nc.tensor.matmul(
-            mod_flat, lhsT=eT[:], rhs=mod_w[:].rearrange("k j d -> k (j d)"), start=True, stop=False
-        )
-        nc.tensor.matmul(
-            mod_flat, lhsT=ones[:], rhs=mod_b[:].rearrange("k j d -> k (j d)"), start=False, stop=True
-        )
         gate = consts.tile([P, DO], F32)
         scale = consts.tile([P, DO], F32)
-        nc.scalar.activation(out=gate[:], in_=mod_ps[:, 0, :], func=ACT.Sigmoid)
-        nc.scalar.activation(out=scale[:], in_=mod_ps[:, 1, :], func=ACT.Tanh)
         factor = consts.tile([P, DO], F32)
         shift_gate = consts.tile([P, DO], F32)
         offset = consts.tile([P, DO], F32)
-        nc.vector.scalar_tensor_tensor(
-            out=factor[:], in0=scale[:], scalar=1.0, in1=gate[:], op0=ALU.add, op1=ALU.mult
-        )
-        nc.vector.tensor_tensor(out=shift_gate[:], in0=mod_ps[:, 2, :], in1=gate[:], op=ALU.mult)
-        nc.vector.tensor_tensor(out=offset[:], in0=mod_ps[:, 3, :], in1=factor[:], op=ALU.mult)
-        nc.vector.tensor_tensor(out=offset[:], in0=offset[:], in1=shift_gate[:], op=ALU.add)
         factor_rows = factor[:].unsqueeze(1).to_broadcast([P, BANK_ROWS, DO])
         offset_rows = offset[:].unsqueeze(1).to_broadcast([P, BANK_ROWS, DO])
+
+        eT = consts.tile([P, P], BF16)
+
+        def transpose_edge_features():
+            eT_ps = xt_pool.tile([P, P], BF16, tag="xt")
+            nc.tensor.transpose(eT_ps[:], e_sb[:], ident_bf16[:])
+            nc.vector.tensor_copy(out=eT[:], in_=eT_ps[:])
+
+        def make_factor_and_offset():
+            mod_ps = xt_pool.tile([P, 4, DO], F32, tag="xt")
+            mod_flat = mod_ps[:].rearrange("b j d -> b (j d)")
+            nc.tensor.matmul(
+                mod_flat, lhsT=eT[:], rhs=mod_w[:].rearrange("k j d -> k (j d)"), start=True, stop=False
+            )
+            nc.tensor.matmul(
+                mod_flat, lhsT=ones[:], rhs=mod_b[:].rearrange("k j d -> k (j d)"), start=False, stop=True
+            )
+            nc.scalar.activation(out=gate[:], in_=mod_ps[:, 0, :], func=ACT.Sigmoid)
+            nc.scalar.activation(out=scale[:], in_=mod_ps[:, 1, :], func=ACT.Tanh)
+            nc.vector.scalar_tensor_tensor(
+                out=factor[:], in0=scale[:], scalar=1.0, in1=gate[:], op0=ALU.add, op1=ALU.mult
+            )
+            nc.vector.tensor_tensor(out=shift_gate[:], in0=mod_ps[:, 2, :], in1=gate[:], op=ALU.mult)
+            nc.vector.tensor_tensor(out=offset[:], in0=mod_ps[:, 3, :], in1=factor[:], op=ALU.mult)
+            nc.vector.tensor_tensor(out=offset[:], in0=offset[:], in1=shift_gate[:], op=ALU.add)
 
         rows_tiles = {}
 
@@ -198,6 +206,8 @@ def tile_graphditunit_pa_t_kernel(
             k, part = divmod(u, UNITS_PER_BANK)
             if ahead < UNITS:
                 transpose_unit(ahead)
+            if u == 0:
+                transpose_edge_features()
             if part == 0:
                 acc = acc_pool.tile([P, BANK_ROWS, DO], F32, tag="acc")
             multiply_unit(u, acc)
@@ -207,5 +217,7 @@ def tile_graphditunit_pa_t_kernel(
                 scale_bank(k, acc)
             if ahead < UNITS:
                 quantise_unit(ahead)
+            if u == 0:
+                make_factor_and_offset()
         shift_and_store_bank(BANKS - 2)
         shift_and_store_bank(BANKS - 1)

from contextlib import ExitStack

import concourse.mybir as mybir
from concourse.masks import make_identity

F32 = mybir.dt.float32
BF16 = mybir.dt.bfloat16
U32 = mybir.dt.uint32
U8 = mybir.dt.uint8
FP8X4 = mybir.dt.float8_e4m3fn_x4
ACT = mybir.ActivationFunctionType
ALU = mybir.AluOpType

P = 128
ROWS = 64
D = 1024
DO = 128
E = 128

PACK = 4
PASSES = D // (P * PACK)
PAIRS = 2
WORD_BLOCKS = PASSES * PAIRS

LOAD_ROWS = 4
SMALL_ROWS = 2
SMALL_LOADS = 4
LARGE_LOADS = (ROWS - SMALL_LOADS * SMALL_ROWS) // LOAD_ROWS
BANK_ROWS = 4
BANKS = ROWS // BANK_ROWS
UNIT_ROWS = 2
UNITS = ROWS // UNIT_ROWS
UNITS_PER_BANK = BANK_ROWS // UNIT_ROWS
XT_BANKS = 6
ACC_BANKS = 2
LEAD = XT_BANKS // UNIT_ROWS

FLOPS = 2 * P * ROWS * D * DO + 3 * 2 * P * E * DO


def tile_graphditunit_pa_t_kernel(
    tc, x, edge_features, Wv, bv, Wgate, bgate, Wscale, bscale, Wshift, bshift, out
):
    nc = tc.nc
    with ExitStack() as ctx:
        ctx.enter_context(tc.manual_schedule())
        consts = ctx.enter_context(tc.tile_pool(name="consts", bufs=1))
        x_pool = ctx.enter_context(tc.tile_pool(name="x_pool", bufs=1))
        rows_pool = ctx.enter_context(tc.tile_pool(name="rows_pool", bufs=BANKS))
        unit_pool = ctx.enter_context(tc.tile_pool(name="unit_pool", bufs=LEAD + 2))
        xt_pool = ctx.enter_context(tc.psum_pool(name="xt_pool", bufs=XT_BANKS))
        acc_pool = ctx.enter_context(tc.psum_pool(name="acc_pool", bufs=ACC_BANKS))

        ident_f32 = consts.tile([P, P], F32)
        make_identity(nc, ident_f32[:])
        ident_bf16 = consts.tile([P, P], BF16)
        ones = consts.tile([P, P], BF16)
        mod_w = consts.tile([P, 4, DO], BF16)
        mod_b = consts.tile([P, 4, DO], BF16)
        nc.vector.memset(mod_b[:], 0.0)
        nc.vector.memset(mod_w[:, 3, :], 0.0)
        nc.vector.memset(ones[:], 1.0)
        nc.vector.tensor_copy(out=ident_bf16[:], in_=ident_f32[:])
        table_warmer = consts.tile([P, 1], F32)
        nc.scalar.activation(out=table_warmer[:], in_=ident_f32[:, 0:1], func=ACT.Sigmoid)

        x_rows = {}

        def load_x(first, rows):
            x_sb = x_pool.tile([P, rows, D], BF16, tag="x%d" % rows, bufs=SMALL_LOADS if rows == SMALL_ROWS else LARGE_LOADS)
            nc.sync.dma_start(out=x_sb[:], in_=x[:, first : first + rows, :])
            for r in range(rows):
                x_rows[first + r] = (x_sb, r)

        load_x(0, SMALL_ROWS)
        load_x(SMALL_ROWS, SMALL_ROWS)
        w_raw = consts.tile([P, PASSES, PACK, DO], BF16)
        nc.sync.dma_start(
            out=w_raw[:].rearrange("q g t d -> q g (t d)"),
            in_=Wv.rearrange("(g q t) d -> q g (t d)", g=PASSES, t=PACK),
        )
        load_x(2 * SMALL_ROWS, SMALL_ROWS)
        load_x(3 * SMALL_ROWS, SMALL_ROWS)
        e_sb = consts.tile([P, E], BF16)
        nc.sync.dma_start(out=e_sb[:], in_=edge_features[:, :])
        nc.sync.dma_start(out=mod_w[:, 0, :], in_=Wgate[:, :])
        nc.sync.dma_start(out=mod_w[:, 1, :], in_=Wscale[:, :])
        nc.sync.dma_start(out=mod_w[:, 2, :], in_=Wshift[:, :])
        for first in range(SMALL_LOADS * SMALL_ROWS, ROWS, LOAD_ROWS):
            load_x(first, LOAD_ROWS)
        for j, bias in enumerate((bgate, bscale, bshift, bv)):
            nc.gpsimd.dma_start(out=mod_b[0:1, j, :], in_=bias.unsqueeze(0))

        w_grouped = consts.tile([P, PASSES, DO, PACK], BF16, align_bytes=64)
        w_codes = consts.tile([P, PASSES, DO], U32, align_bytes=64)
        w_scales = consts.tile([P, PASSES, DO], U8, align_bytes=64)
        nc.vector.tensor_copy(out=w_grouped[:], in_=w_raw[:].rearrange("q g t d -> q g d t"))

        grouped_tiles = {}
        quantised = {}

        def transpose_unit(u):
            grouped = unit_pool.tile([P, UNIT_ROWS, PASSES, P, PACK], BF16, align_bytes=64)
            grouped_words = grouped[:].bitcast(F32)
            for r in range(UNIT_ROWS):
                x_sb, row = x_rows[u * UNIT_ROWS + r]
                x_words = x_sb[:].bitcast(F32)
                xt = xt_pool.tile([P, WORD_BLOCKS, P], F32, tag="xt")
                for j in range(WORD_BLOCKS):
                    g, h = divmod(j, PAIRS)
                    first = g * PAIRS * P + h
                    nc.tensor.transpose(
                        xt[:, j, :],
                        x_words[:, row, first : (g + 1) * PAIRS * P : PAIRS],
                        ident_f32[:],
                    )
                nc.scalar.copy(
                    out=grouped_words[:, r],
                    in_=xt[:].rearrange("q (g h) b -> q g b h", g=PASSES),
                )
            grouped_tiles[u] = grouped

        def quantise_unit(u):
            codes = unit_pool.tile([P, UNIT_ROWS, PASSES, P], U32, align_bytes=64)
            scales = unit_pool.tile([P, UNIT_ROWS, PASSES, P], U8, align_bytes=64)
            nc.vector.quantize_mx(
                out=codes[:].rearrange("q r g b -> q (r g b)").bitcast(FP8X4),
                scales=scales[:].rearrange("q r g b -> q (r g b)"),
                in_=grouped_tiles[u][:].rearrange("q r g b t -> q (r g b t)"),
            )
            quantised[u] = (codes, scales)

        def multiply_unit(u, acc):
            codes, scales = quantised[u]
            for r in range(UNIT_ROWS):
                bank_row = (u % UNITS_PER_BANK) * UNIT_ROWS + r
                for g in range(PASSES):
                    nc.tensor.matmul_mx(
                        out=acc[:, bank_row, :],
                        lhsT=codes[:, r, g, :].bitcast(FP8X4),
                        lhsT_scale=scales[:, r, g, :],
                        rhs=w_codes[:, g, :].bitcast(FP8X4),
                        rhs_scale=w_scales[:, g, :],
                        start=(g == 0),
                        stop=(g == PASSES - 1),
                    )

        for u in range(LEAD):
            transpose_unit(u)
            quantise_unit(u)
            if u == 0:
                nc.vector.quantize_mx(
                    out=w_codes[:].rearrange("q g d -> q (g d)").bitcast(FP8X4),
                    scales=w_scales[:].rearrange("q g d -> q (g d)"),
                    in_=w_grouped[:].rearrange("q g d t -> q (g d t)"),
                )

        gate = consts.tile([P, DO], F32)
        scale = consts.tile([P, DO], F32)
        factor = consts.tile([P, DO], F32)
        shift_gate = consts.tile([P, DO], F32)
        offset = consts.tile([P, DO], F32)
        factor_rows = factor[:].unsqueeze(1).to_broadcast([P, BANK_ROWS, DO])
        offset_rows = offset[:].unsqueeze(1).to_broadcast([P, BANK_ROWS, DO])

        eT = consts.tile([P, P], BF16)

        def transpose_edge_features():
            eT_ps = xt_pool.tile([P, P], BF16, tag="xt")
            nc.tensor.transpose(eT_ps[:], e_sb[:], ident_bf16[:])
            nc.vector.tensor_copy(out=eT[:], in_=eT_ps[:])

        def make_factor_and_offset():
            mod_ps = xt_pool.tile([P, 4, DO], F32, tag="xt")
            mod_flat = mod_ps[:].rearrange("b j d -> b (j d)")
            nc.tensor.matmul(
                mod_flat, lhsT=eT[:], rhs=mod_w[:].rearrange("k j d -> k (j d)"), start=True, stop=False
            )
            nc.tensor.matmul(
                mod_flat, lhsT=ones[:], rhs=mod_b[:].rearrange("k j d -> k (j d)"), start=False, stop=True
            )
            nc.scalar.activation(out=gate[:], in_=mod_ps[:, 0, :], func=ACT.Sigmoid)
            nc.scalar.activation(out=scale[:], in_=mod_ps[:, 1, :], func=ACT.Tanh)
            nc.vector.scalar_tensor_tensor(
                out=factor[:], in0=scale[:], scalar=1.0, in1=gate[:], op0=ALU.add, op1=ALU.mult
            )
            nc.vector.tensor_tensor(out=shift_gate[:], in0=mod_ps[:, 2, :], in1=gate[:], op=ALU.mult)
            nc.vector.tensor_tensor(out=offset[:], in0=mod_ps[:, 3, :], in1=factor[:], op=ALU.mult)
            nc.vector.tensor_tensor(out=offset[:], in0=offset[:], in1=shift_gate[:], op=ALU.add)

        rows_tiles = {}

        def scale_bank(k, acc):
            rows = rows_pool.tile([P, BANK_ROWS, DO], F32)
            nc.vector.tensor_tensor(out=rows[:], in0=acc[:], in1=factor_rows, op=ALU.mult)
            rows_tiles[k] = rows

        def shift_and_store_bank(k):
            rows = rows_tiles[k]
            nc.vector.tensor_tensor(out=rows[:], in0=rows[:], in1=offset_rows, op=ALU.add)
            nc.sync.dma_start(out=out[:, k * BANK_ROWS : (k + 1) * BANK_ROWS, :], in_=rows[:])

        acc = None
        for u in range(UNITS):
            ahead = u + LEAD
            k, part = divmod(u, UNITS_PER_BANK)
            if ahead < UNITS:
                transpose_unit(ahead)
            if u == 0:
                transpose_edge_features()
            if part == 0:
                acc = acc_pool.tile([P, BANK_ROWS, DO], F32, tag="acc")
            multiply_unit(u, acc)
            if part == 0 and 0 < k < BANKS - 1:
                shift_and_store_bank(k - 1)
            if part == UNITS_PER_BANK - 1:
                scale_bank(k, acc)
            if ahead < UNITS:
                quantise_unit(ahead)
            if u == 0:
                make_factor_and_offset()
        shift_and_store_bank(BANKS - 2)
        shift_and_store_bank(BANKS - 1)
